import numpy as np
import ml_dtypes


def mxq(x, axis, fmt="e4m3"):
    dtype, down = {"e4m3": (ml_dtypes.float8_e4m3fn, 7), "e5m2": (ml_dtypes.float8_e5m2, 14)}[fmt]
    v = np.moveaxis(np.asarray(x, np.float32).astype(ml_dtypes.bfloat16).astype(np.float64), axis, -1)
    blocks = v.reshape(v.shape[:-1] + (-1, 32))
    amax = np.abs(blocks).max(-1, keepdims=True)
    byte = np.maximum(np.where(amax > 0, np.frexp(amax)[1] - 1 + 127, 0) - down, 1)
    scale = np.exp2(byte - 127.0)
    codes = (blocks / scale).astype(np.float32).astype(dtype).astype(np.float64)
    return np.moveaxis((codes * scale).reshape(v.shape), -1, axis)


WIDE = False


def mx_kscale(k):
    if not WIDE:
        return np.ones(k)
    levels = np.array([10, -10, 5, -5, 0])
    a = np.random.permutation(np.resize(levels, k // 512 * 4)).reshape(k // 512, 4)
    idx = np.arange(k)
    return np.exp2(a[idx // 512, idx % 128 // 32])


BF16 = ml_dtypes.bfloat16


def bf(x):
    return np.asarray(x, np.float32).astype(BF16)


def f64(x):
    return np.asarray(x).astype(np.float64)


E, H, F = 4, 512, 3072
N = 256


def erf(v):
    a = np.clip(v, -6.0, 6.0)
    a2 = 2.0 * a * a
    term = a.copy()
    tot = a.copy()
    for n in range(1, 110):
        term = term * a2 / (2 * n + 1)
        tot = tot + term
    return 2.0 / np.sqrt(np.pi) * np.exp(-a * a) * tot


def gelu_exact(v):
    return 0.5 * v * (1.0 + erf(v / np.sqrt(2.0)))


def setup_inputs():
    s = mx_kscale(H)
    idx = np.arange(E, dtype=np.float64)
    scale = 1.0 + (idx - E // 2) * 0.01
    hidden_states = np.random.standard_normal((N, H)) * s
    Wi = np.random.standard_normal((E, H, F)) * 0.044 * scale[:, None, None] / s[None, :, None]
    bi = np.random.standard_normal((E, F)) * 0.1 + (idx - E // 2)[:, None] * 0.001
    Wo = np.random.standard_normal((E, F, H)) * 0.03
    bo = np.random.standard_normal((E, H)) * 0.1
    return {"hidden_states": bf(hidden_states), "Wi": bf(Wi), "bi": bf(bi), "Wo": bf(Wo), "bo": bf(bo)}


def reference(hidden_states, Wi, bi, Wo, bo):
    inter = (mxq(f64(hidden_states), 1, "e4m3") @ mxq(f64(Wi), 1, "e4m3")) + f64(bi)[:, None, :]
    inter = gelu_exact(inter)
    out = (mxq(inter, 2, "e4m3") @ mxq(f64(Wo), 1, "e4m3")) + f64(bo)[:, None, :]
    return out

@@ -1,0 +1,209 @@
+from contextlib import ExitStack
+
+import concourse.mybir as mybir
+from concourse.masks import make_identity
+
+F32 = mybir.dt.float32
+BF16 = mybir.dt.bfloat16
+U32 = mybir.dt.uint32
+U8 = mybir.dt.uint8
+FP8X4 = mybir.dt.float8_e4m3fn_x4
+ACT = mybir.ActivationFunctionType
+ALU = mybir.AluOpType
+
+E, H, F, N = 4, 512, 3072, 256
+P = 128
+FLOPS = 2 * E * N * H * F * 2
+
+UNITS = 3
+G = E * UNITS
+RAW_BUFS = 10
+XI = 528
+XO = 264
+
+
+def tile_bertmoeexpertpool_kernel(tc, hidden_states, Wi, bi, Wo, bo, out):
+    nc = tc.nc
+    with ExitStack() as ctx:
+        const = ctx.enter_context(tc.tile_pool(name="const", bufs=1))
+        rawp = ctx.enter_context(tc.tile_pool(name="raw", bufs=RAW_BUFS))
+        grp = ctx.enter_context(tc.tile_pool(name="grp", bufs=2))
+        cod = ctx.enter_context(tc.tile_pool(name="cod", bufs=3))
+        act = ctx.enter_context(tc.tile_pool(name="act", bufs=3))
+        res = ctx.enter_context(tc.tile_pool(name="res", bufs=4))
+        ps_h = ctx.enter_context(tc.psum_pool(name="ps_h", bufs=4))
+        ps_o = ctx.enter_context(tc.psum_pool(name="ps_o", bufs=4))
+
+        raw = {}
+        grouped = {}
+        codes = {}
+        planes = {}
+        gelu_out = {}
+        acc = {}
+
+        def load(s):
+            if s >= 2 * G:
+                return
+            g, kind = s // 2, s % 2
+            e, u = g // UNITS, g % UNITS
+            t = rawp.tile([P, 4096], BF16, name="raw_t", tag="raw")
+            if kind == 0:
+                nc.sync.dma_start(
+                    out=t[:].rearrange("p (j w) -> p j w", j=4),
+                    in_=Wi[e].rearrange("(p j) f -> p j f", j=4)[:, :, u * 1024 : (u + 1) * 1024],
+                )
+            else:
+                nc.sync.dma_start(
+                    out=t[:].rearrange("p (r h) -> p r h", r=8),
+                    in_=Wo[e, u * 1024 : (u + 1) * 1024, :].rearrange("(r p) h -> p r h", p=P),
+                )
+            raw[(g, kind)] = t
+
+        def regroup_wi(g):
+            if g < 0 or g >= G:
+                return
+            src = raw[(g, 0)][:].rearrange("p (j w) -> p w j", j=4)
+            t = grp.tile([P, 1024, 4], BF16, name="grp_i", tag="grp_i", align_bytes=64)
+            nc.vector.tensor_copy(out=t[:, 0:XI, :], in_=src[:, 0:XI, :])
+            nc.scalar.copy(out=t[:, XI:1024, :], in_=src[:, XI:1024, :])
+            grouped[(g, 0)] = t[:].rearrange("p w j -> p (w j)")
+
+        def regroup_wo(g):
+            if g < 0 or g >= G:
+                return
+            src = raw[(g, 1)][:].rearrange("p (c t h) -> p c h t", c=2, t=4)
+            t = grp.tile([P, 2, 512, 4], BF16, name="grp_o", tag="grp_o", align_bytes=64)
+            nc.vector.tensor_copy(out=t[:, :, 0:XO, :], in_=src[:, :, 0:XO, :])
+            nc.scalar.copy(out=t[:, :, XO:512, :], in_=src[:, :, XO:512, :])
+            grouped[(g, 1)] = t[:].rearrange("p c w j -> p (c w j)")
+
+        def quantise(key, width, tag):
+            words = cod.tile([P, width], U32, name="w_" + tag, tag="w_" + tag, align_bytes=64)
+            plane = cod.tile([P, width], U8, name="s_" + tag, tag="s_" + tag, align_bytes=64)
+            nc.vector.quantize_mx(out=words[:].bitcast(FP8X4), scales=plane[:], in_=grouped[key])
+            codes[key] = words
+            planes[key] = plane
+
+        def quant_wi(g):
+            if 0 <= g < G:
+                quantise((g, 0), 1024, "i")
+
+        def quant_wo(g):
+            if 0 <= g < G:
+                quantise((g, 1), 1024, "o")
+
+        def first_matmul_and_gelu(g):
+            if g < 0 or g >= G:
+                return
+            e, u = g // UNITS, g % UNITS
+            t = act.tile([P, 2, 4, N], BF16, name="gelu_t", tag="gelu_t")
+            for i in range(8):
+                cols = slice(i * P, (i + 1) * P)
+                h_ps = ps_h.tile([P, N], F32, name="h_ps", tag="h_ps")
+                nc.tensor.matmul_mx(
+                    out=h_ps[:],
+                    lhsT=codes[(g, 0)][:, cols].bitcast(FP8X4),
+                    lhsT_scale=planes[(g, 0)][:, cols],
+                    rhs=x_words[:].bitcast(FP8X4),
+                    rhs_scale=x_plane[:],
+                    start=True,
+                    stop=True,
+                )
+                col = e * 24 + u * 8 + i
+                nc.scalar.activation(
+                    out=t[:, i // 4, i % 4, :], in_=h_ps[:], func=ACT.Gelu, bias=bi_t[:, col : col + 1], scale=1.0
+                )
+            gelu_out[g] = t
+
+        def regroup_inter(g):
+            if g < 0 or g >= G:
+                return
+            t = act.tile([P, 2, N, 4], BF16, name="grp_a", tag="grp_a", align_bytes=64)
+            nc.vector.tensor_copy(out=t[:], in_=gelu_out[g][:].rearrange("p c t n -> p c n t"))
+            grouped[(g, 2)] = t[:].rearrange("p c w j -> p (c w j)")
+
+        def quant_inter(g):
+            if 0 <= g < G:
+                quantise((g, 2), 2 * N, "a")
+
+        def second_matmul(g):
+            if g < 0 or g >= G:
+                return
+            e, u = g // UNITS, g % UNITS
+            if u == 0:
+                for a in range(2):
+                    acc[(e, a)] = ps_o.tile([P, H], F32, name="o_ps", tag="o_ps")
+            for a in range(2):
+                for c in range(2):
+                    toks = slice(c * N + a * P, c * N + (a + 1) * P)
+                    nc.tensor.matmul_mx(
+                        out=acc[(e, a)][:],
+                        lhsT=codes[(g, 2)][:, toks].bitcast(FP8X4),
+                        lhsT_scale=planes[(g, 2)][:, toks],
+                        rhs=codes[(g, 1)][:, c * H : (c + 1) * H].bitcast(FP8X4),
+                        rhs_scale=planes[(g, 1)][:, c * H : (c + 1) * H],
+                        start=(u == 0 and c == 0),
+                        stop=(u == UNITS - 1 and c == 1),
+                    )
+            if u == UNITS - 1:
+                for a in range(2):
+                    o_sb = res.tile([P, H], F32, name="o_sb", tag="o_sb")
+                    nc.vector.tensor_tensor(
+                        out=o_sb[:], in0=acc[(e, a)][:], in1=bo_bc[:, e * H : (e + 1) * H], op=ALU.add
+                    )
+                    queue = nc.sync if e == E - 1 else nc.gpsimd
+                    queue.dma_start(out=out[e, a * P : (a + 1) * P, :], in_=o_sb[:])
+
+        x_sb = const.tile([P, 2, H], BF16, name="x_sb")
+        nc.sync.dma_start(out=x_sb[:], in_=hidden_states.rearrange("(a p) k -> p a k", p=P))
+        bi_rows = const.tile([P, P], BF16, name="bi_rows")
+        nc.vector.memset(bi_rows[:], 0.0)
+        nc.sync.dma_start(out=bi_rows[0:96, :], in_=bi.rearrange("e (t p) -> (e t) p", p=P))
+        for s in range(2):
+            load(s)
+        bo_bc = const.tile([P, E * H], BF16, name="bo_bc")
+        nc.sync.dma_start(out=bo_bc[:], in_=bo.rearrange("e h -> (e h)").partition_broadcast(P))
+        for s in range(2, RAW_BUFS):
+            load(s)
+        next_load = [RAW_BUFS]
+
+        ident = const.tile([P, P], F32, name="ident")
+        make_identity(nc, ident[:])
+        warm = const.tile([P, 1], F32, name="warm")
+        nc.vector.memset(warm[:], 0.0)
+        nc.scalar.activation(out=warm[:], in_=warm[:], func=ACT.Gelu)
+
+        x_ps = ps_o.tile([P, 2, N], F32, name="x_ps", tag="o_ps")
+        for a in range(2):
+            words = x_sb[:, a, :].bitcast(F32).rearrange("p (q u) -> p u q", u=2)
+            for u in range(2):
+                nc.tensor.transpose(x_ps[:, u, a * P : (a + 1) * P], words[:, u, :], ident[:])
+        x_grp = const.tile([P, 4 * N], BF16, name="x_grp", align_bytes=64)
+        nc.vector.tensor_copy(
+            out=x_grp[:].bitcast(F32).rearrange("p (n u) -> p n u", u=2), in_=x_ps[:].rearrange("p u n -> p n u")
+        )
+        bi_f = const.tile([P, P], F32, name="bi_f")
+        nc.vector.tensor_copy(out=bi_f[:], in_=bi_rows[:])
+        x_words = const.tile([P, N], U32, name="x_words", align_bytes=64)
+        x_plane = const.tile([P, N], U8, name="x_plane", align_bytes=64)
+        nc.vector.quantize_mx(out=x_words[:].bitcast(FP8X4), scales=x_plane[:], in_=x_grp[:])
+        bi_ps = ps_h.tile([P, P], F32, name="bi_ps", tag="h_ps")
+        nc.tensor.transpose(bi_ps[:], bi_f[:], ident[:])
+        bi_t = const.tile([P, P], F32, name="bi_t")
+        nc.vector.tensor_copy(out=bi_t[:], in_=bi_ps[:])
+
+        for i in range(-1, G + 1):
+            quant_wi(i)
+            regroup_wi(i + 1)
+            if i + 1 < G:
+                load(next_load[0])
+                next_load[0] += 1
+            first_matmul_and_gelu(i)
+            quant_wo(i)
+            regroup_inter(i - 1)
+            regroup_wo(i + 1)
+            if i + 1 < G:
+                load(next_load[0])
+                next_load[0] += 1
+            quant_inter(i - 1)
+            second_matmul(i - 1)

@@ -33,6 +33,7 @@ def tile_bertmoeexpertpool_kernel(tc, hidden_states, Wi, bi, Wo, bo, out):
         res = ctx.enter_context(tc.tile_pool(name="res", bufs=4))
         ps_h = ctx.enter_context(tc.psum_pool(name="ps_h", bufs=4))
         ps_o = ctx.enter_context(tc.psum_pool(name="ps_o", bufs=4))
+        ctx.enter_context(tc.manual_schedule())
 
         raw = {}
         grouped = {}

@@ -15,11 +15,11 @@ E, H, F, N = 4, 512, 3072, 256
 P = 128
 FLOPS = 2 * E * N * H * F * 2
 
-UNITS = 3
-G = E * UNITS
+K_UNITS = 24
 RAW_BUFS = 10
-XI = 528
-XO = 264
+SPLIT = [1920,2560,3136,2880,1024,2048]
+SPLIT_AT = {1: 3200, 2: 3200, 20: 3136, 21: 2944, 23: 1920}
+HEAD = ["V","S","V","V"]
 
 
 def tile_bertmoeexpertpool_kernel(tc, hidden_states, Wi, bi, Wo, bo, out):
@@ -27,12 +27,14 @@ def tile_bertmoeexpertpool_kernel(tc, hidden_states, Wi, bi, Wo, bo, out):
     with ExitStack() as ctx:
         const = ctx.enter_context(tc.tile_pool(name="const", bufs=1))
         rawp = ctx.enter_context(tc.tile_pool(name="raw", bufs=RAW_BUFS))
-        grp = ctx.enter_context(tc.tile_pool(name="grp", bufs=2))
-        cod = ctx.enter_context(tc.tile_pool(name="cod", bufs=3))
+        headp = ctx.enter_context(tc.tile_pool(name="head", bufs=4))
+        grp = ctx.enter_context(tc.tile_pool(name="grp", bufs=3))
+        cod = ctx.enter_context(tc.tile_pool(name="cod", bufs=4))
+        cod_a = ctx.enter_context(tc.tile_pool(name="cod_a", bufs=6))
         act = ctx.enter_context(tc.tile_pool(name="act", bufs=3))
         res = ctx.enter_context(tc.tile_pool(name="res", bufs=4))
-        ps_h = ctx.enter_context(tc.psum_pool(name="ps_h", bufs=4))
-        ps_o = ctx.enter_context(tc.psum_pool(name="ps_o", bufs=4))
+        ps_h = ctx.enter_context(tc.psum_pool(name="ps_h", bufs=6))
+        ps_o = ctx.enter_context(tc.psum_pool(name="ps_o", bufs=2))
         ctx.enter_context(tc.manual_schedule())
 
         raw = {}
@@ -41,96 +43,116 @@ def tile_bertmoeexpertpool_kernel(tc, hidden_states, Wi, bi, Wo, bo, out):
         planes = {}
         gelu_out = {}
         acc = {}
+        next_load = [0]
 
-        def load(s):
-            if s >= 2 * G:
+        def is_wi(k):
+            return 0 <= k < K_UNITS and k % 6 < 3
+
+        def is_wo(k):
+            return 0 <= k < K_UNITS and k % 6 >= 3
+
+        def wi_rows(k):
+            return Wi[k // 6].rearrange("(p j) f -> p j f", j=4)
+
+        def load():
+            k = next_load[0]
+            next_load[0] += 1
+            if k >= K_UNITS:
                 return
-            g, kind = s // 2, s % 2
-            e, u = g // UNITS, g % UNITS
+            e, u = k // 6, k % 3
             t = rawp.tile([P, 4096], BF16, name="raw_t", tag="raw")
-            if kind == 0:
+            if is_wi(k):
                 nc.sync.dma_start(
-                    out=t[:].rearrange("p (j w) -> p j w", j=4),
-                    in_=Wi[e].rearrange("(p j) f -> p j f", j=4)[:, :, u * 1024 : (u + 1) * 1024],
+                    out=t[:].rearrange("p (j w) -> p j w", j=4), in_=wi_rows(k)[:, :, u * 1024 : (u + 1) * 1024]
                 )
             else:
                 nc.sync.dma_start(
                     out=t[:].rearrange("p (r h) -> p r h", r=8),
                     in_=Wo[e, u * 1024 : (u + 1) * 1024, :].rearrange("(r p) h -> p r h", p=P),
                 )
-            raw[(g, kind)] = t
+            raw[k] = t
 
-        def regroup_wi(g):
-            if g < 0 or g >= G:
+        def copy_on(engine, dst, src):
+            if engine == "V":
+                nc.vector.tensor_copy(out=dst, in_=src)
+            else:
+                nc.scalar.copy(out=dst, in_=src)
+
+        def regroup(k):
+            if k < 0 or k >= K_UNITS:
                 return
-            src = raw[(g, 0)][:].rearrange("p (j w) -> p w j", j=4)
-            t = grp.tile([P, 1024, 4], BF16, name="grp_i", tag="grp_i", align_bytes=64)
-            nc.vector.tensor_copy(out=t[:, 0:XI, :], in_=src[:, 0:XI, :])
-            nc.scalar.copy(out=t[:, XI:1024, :], in_=src[:, XI:1024, :])
-            grouped[(g, 0)] = t[:].rearrange("p w j -> p (w j)")
+            t = grp.tile([P, 4096], BF16, name="grp_t", tag="grp_t", align_bytes=64)
+            grouped[k] = t
+            share = SPLIT_AT.get(k, SPLIT[k % 6])
+            if k == 0:
+                dst = t[:].rearrange("p (w j) -> p w j", j=4)
+                for q in range(4):
+                    copy_on(HEAD[q], dst[:, q * 256 : (q + 1) * 256, :], raw[(0, q)][:].rearrange("p j w -> p w j"))
+            elif is_wi(k):
+                x = share // 4
+                dst = t[:].rearrange("p (w j) -> p w j", j=4)
+                src = raw[k][:].rearrange("p (j w) -> p w j", j=4)
+                copy_on("V", dst[:, 0:x, :], src[:, 0:x, :])
+                copy_on("S", dst[:, x:1024, :], src[:, x:1024, :])
+                load()
+            else:
+                x = share // 8
+                dst = t[:].rearrange("p (c h j) -> p c h j", c=2, j=4)
+                src = raw[k][:].rearrange("p (c j h) -> p c h j", c=2, j=4)
+                copy_on("V", dst[:, :, 0:x, :], src[:, :, 0:x, :])
+                copy_on("S", dst[:, :, x:512, :], src[:, :, x:512, :])
+                load()
 
-        def regroup_wo(g):
-            if g < 0 or g >= G:
-                return
-            src = raw[(g, 1)][:].rearrange("p (c t h) -> p c h t", c=2, t=4)
-            t = grp.tile([P, 2, 512, 4], BF16, name="grp_o", tag="grp_o", align_bytes=64)
-            nc.vector.tensor_copy(out=t[:, :, 0:XO, :], in_=src[:, :, 0:XO, :])
-            nc.scalar.copy(out=t[:, :, XO:512, :], in_=src[:, :, XO:512, :])
-            grouped[(g, 1)] = t[:].rearrange("p c w j -> p (c w j)")
-
-        def quantise(key, width, tag):
-            words = cod.tile([P, width], U32, name="w_" + tag, tag="w_" + tag, align_bytes=64)
-            plane = cod.tile([P, width], U8, name="s_" + tag, tag="s_" + tag, align_bytes=64)
-            nc.vector.quantize_mx(out=words[:].bitcast(FP8X4), scales=plane[:], in_=grouped[key])
+        def quantise(pool, key, width, tag):
+            words = pool.tile([P, width], U32, name="w_" + tag, tag="w_" + tag, align_bytes=64)
+            plane = pool.tile([P, width], U8, name="s_" + tag, tag="s_" + tag, align_bytes=64)
+            nc.vector.quantize_mx(out=words[:].bitcast(FP8X4), scales=plane[:], in_=grouped[key][:])
             codes[key] = words
             planes[key] = plane
 
-        def quant_wi(g):
-            if 0 <= g < G:
-                quantise((g, 0), 1024, "i")
+        def quant_weights(k):
+            if 0 <= k < K_UNITS:
+                quantise(cod, k, 1024, "w")
 
-        def quant_wo(g):
-            if 0 <= g < G:
-                quantise((g, 1), 1024, "o")
-
-        def first_matmul_and_gelu(g):
-            if g < 0 or g >= G:
+        def first_matmul_and_gelu(k):
+            if not is_wi(k):
                 return
-            e, u = g // UNITS, g % UNITS
             t = act.tile([P, 2, 4, N], BF16, name="gelu_t", tag="gelu_t")
             for i in range(8):
                 cols = slice(i * P, (i + 1) * P)
                 h_ps = ps_h.tile([P, N], F32, name="h_ps", tag="h_ps")
                 nc.tensor.matmul_mx(
                     out=h_ps[:],
-                    lhsT=codes[(g, 0)][:, cols].bitcast(FP8X4),
-                    lhsT_scale=planes[(g, 0)][:, cols],
+                    lhsT=codes[k][:, cols].bitcast(FP8X4),
+                    lhsT_scale=planes[k][:, cols],
                     rhs=x_words[:].bitcast(FP8X4),
                     rhs_scale=x_plane[:],
                     start=True,
                     stop=True,
                 )
-                col = e * 24 + u * 8 + i
+                col = (k // 6) * 24 + (k % 3) * 8 + i
                 nc.scalar.activation(
                     out=t[:, i // 4, i % 4, :], in_=h_ps[:], func=ACT.Gelu, bias=bi_t[:, col : col + 1], scale=1.0
                 )
-            gelu_out[g] = t
+            gelu_out[k] = t
 
-        def regroup_inter(g):
-            if g < 0 or g >= G:
+        def regroup_inter(k):
+            if not is_wi(k):
                 return
-            t = act.tile([P, 2, N, 4], BF16, name="grp_a", tag="grp_a", align_bytes=64)
-            nc.vector.tensor_copy(out=t[:], in_=gelu_out[g][:].rearrange("p c t n -> p c n t"))
-            grouped[(g, 2)] = t[:].rearrange("p c w j -> p (c w j)")
+            t = act.tile([P, 2048], BF16, name="grp_a", tag="grp_a", align_bytes=64)
+            nc.vector.tensor_copy(
+                out=t[:].rearrange("p (c n j) -> p c n j", c=2, j=4), in_=gelu_out[k][:].rearrange("p c j n -> p c n j")
+            )
+            grouped[("a", k)] = t
 
-        def quant_inter(g):
-            if 0 <= g < G:
-                quantise((g, 2), 2 * N, "a")
+        def quant_inter(k):
+            if is_wi(k):
+                quantise(cod_a, ("a", k), 2 * N, "a")
 
-        def second_matmul(g):
-            if g < 0 or g >= G:
+        def second_matmul(k):
+            if not is_wo(k):
                 return
-            e, u = g // UNITS, g % UNITS
+            e, u = k // 6, k % 3
             if u == 0:
                 for a in range(2):
                     acc[(e, a)] = ps_o.tile([P, H], F32, name="o_ps", tag="o_ps")
@@ -139,34 +161,40 @@ def tile_bertmoeexpertpool_kernel(tc, hidden_states, Wi, bi, Wo, bo, out):
                     toks = slice(c * N + a * P, c * N + (a + 1) * P)
                     nc.tensor.matmul_mx(
                         out=acc[(e, a)][:],
-                        lhsT=codes[(g, 2)][:, toks].bitcast(FP8X4),
-                        lhsT_scale=planes[(g, 2)][:, toks],
-                        rhs=codes[(g, 1)][:, c * H : (c + 1) * H].bitcast(FP8X4),
-                        rhs_scale=planes[(g, 1)][:, c * H : (c + 1) * H],
+                        lhsT=codes[("a", k - 3)][:, toks].bitcast(FP8X4),
+                        lhsT_scale=planes[("a", k - 3)][:, toks],
+                        rhs=codes[k][:, c * H : (c + 1) * H].bitcast(FP8X4),
+                        rhs_scale=planes[k][:, c * H : (c + 1) * H],
                         start=(u == 0 and c == 0),
-                        stop=(u == UNITS - 1 and c == 1),
+                        stop=(u == 2 and c == 1),
                     )
-            if u == UNITS - 1:
-                for a in range(2):
-                    o_sb = res.tile([P, H], F32, name="o_sb", tag="o_sb")
-                    nc.vector.tensor_tensor(
-                        out=o_sb[:], in0=acc[(e, a)][:], in1=bo_bc[:, e * H : (e + 1) * H], op=ALU.add
-                    )
-                    queue = nc.sync if e == E - 1 else nc.gpsimd
-                    queue.dma_start(out=out[e, a * P : (a + 1) * P, :], in_=o_sb[:])
 
+        def add_bo_and_store(k):
+            if not (is_wo(k) and k % 6 == 5):
+                return
+            e = k // 6
+            for a in range(2):
+                o_sb = res.tile([P, H], F32, name="o_sb", tag="o_sb")
+                nc.vector.tensor_tensor(out=o_sb[:], in0=acc[(e, a)][:], in1=bo_bc[:, e * H : (e + 1) * H], op=ALU.add)
+                queue = nc.sync if e == E - 1 else nc.gpsimd
+                queue.dma_start(out=out[e, a * P : (a + 1) * P, :], in_=o_sb[:])
+
+        for q in range(4):
+            piece = headp.tile([P, 4, 256], BF16, name="piece", tag="piece")
+            nc.sync.dma_start(out=piece[:], in_=wi_rows(0)[:, :, q * 256 : (q + 1) * 256])
+            raw[(0, q)] = piece
+        next_load[0] = 1
         x_sb = const.tile([P, 2, H], BF16, name="x_sb")
         nc.sync.dma_start(out=x_sb[:], in_=hidden_states.rearrange("(a p) k -> p a k", p=P))
         bi_rows = const.tile([P, P], BF16, name="bi_rows")
         nc.vector.memset(bi_rows[:], 0.0)
         nc.sync.dma_start(out=bi_rows[0:96, :], in_=bi.rearrange("e (t p) -> (e t) p", p=P))
-        for s in range(2):
-            load(s)
+        load()
+        load()
         bo_bc = const.tile([P, E * H], BF16, name="bo_bc")
         nc.sync.dma_start(out=bo_bc[:], in_=bo.rearrange("e h -> (e h)").partition_broadcast(P))
-        for s in range(2, RAW_BUFS):
-            load(s)
-        next_load = [RAW_BUFS]
+        for s in range(RAW_BUFS - 2):
+            load()
 
         ident = const.tile([P, P], F32, name="ident")
         make_identity(nc, ident[:])
@@ -174,37 +202,34 @@ def tile_bertmoeexpertpool_kernel(tc, hidden_states, Wi, bi, Wo, bo, out):
         nc.vector.memset(warm[:], 0.0)
         nc.scalar.activation(out=warm[:], in_=warm[:], func=ACT.Gelu)
 
-        x_ps = ps_o.tile([P, 2, N], F32, name="x_ps", tag="o_ps")
-        for a in range(2):
-            words = x_sb[:, a, :].bitcast(F32).rearrange("p (q u) -> p u q", u=2)
-            for u in range(2):
-                nc.tensor.transpose(x_ps[:, u, a * P : (a + 1) * P], words[:, u, :], ident[:])
         x_grp = const.tile([P, 4 * N], BF16, name="x_grp", align_bytes=64)
-        nc.vector.tensor_copy(
-            out=x_grp[:].bitcast(F32).rearrange("p (n u) -> p n u", u=2), in_=x_ps[:].rearrange("p u n -> p n u")
-        )
-        bi_f = const.tile([P, P], F32, name="bi_f")
-        nc.vector.tensor_copy(out=bi_f[:], in_=bi_rows[:])
         x_words = const.tile([P, N], U32, name="x_words", align_bytes=64)
         x_plane = const.tile([P, N], U8, name="x_plane", align_bytes=64)
-        nc.vector.quantize_mx(out=x_words[:].bitcast(FP8X4), scales=x_plane[:], in_=x_grp[:])
-        bi_ps = ps_h.tile([P, P], F32, name="bi_ps", tag="h_ps")
-        nc.tensor.transpose(bi_ps[:], bi_f[:], ident[:])
+        bi_f = const.tile([P, P], F32, name="bi_f")
         bi_t = const.tile([P, P], F32, name="bi_t")
-        nc.vector.tensor_copy(out=bi_t[:], in_=bi_ps[:])
 
-        for i in range(-1, G + 1):
-            quant_wi(i)
-            regroup_wi(i + 1)
-            if i + 1 < G:
-                load(next_load[0])
-                next_load[0] += 1
-            first_matmul_and_gelu(i)
-            quant_wo(i)
-            regroup_inter(i - 1)
-            regroup_wo(i + 1)
-            if i + 1 < G:
-                load(next_load[0])
-                next_load[0] += 1
-            quant_inter(i - 1)
-            second_matmul(i - 1)
+        def small_operands():
+            x_ps = ps_o.tile([P, 2, N], F32, name="x_ps", tag="o_ps")
+            for a in range(2):
+                pairs = x_sb[:, a, :].bitcast(F32).rearrange("p (q u) -> p u q", u=2)
+                for u in range(2):
+                    nc.tensor.transpose(x_ps[:, u, a * P : (a + 1) * P], pairs[:, u, :], ident[:])
+            nc.vector.tensor_copy(
+                out=x_grp[:].bitcast(F32).rearrange("p (n u) -> p n u", u=2), in_=x_ps[:].rearrange("p u n -> p n u")
+            )
+            nc.vector.tensor_copy(out=bi_f[:], in_=bi_rows[:])
+            nc.vector.quantize_mx(out=x_words[:].bitcast(FP8X4), scales=x_plane[:], in_=x_grp[:])
+            bi_ps = ps_h.tile([P, P], F32, name="bi_ps", tag="h_ps")
+            nc.tensor.transpose(bi_ps[:], bi_f[:], ident[:])
+            nc.vector.tensor_copy(out=bi_t[:], in_=bi_ps[:])
+
+        for k in range(K_UNITS + 3):
+            if k == 1:
+                small_operands()
+            quant_weights(k - 1)
+            regroup_inter(k - 2)
+            regroup(k)
+            first_matmul_and_gelu(k - 1)
+            second_matmul(k - 1)
+            quant_inter(k - 2)
+            add_bo_and_store(k - 2)

@@ -92,14 +92,22 @@ def tile_bertmoeexpertpool_kernel(tc, hidden_states, Wi, bi, Wo, bo, out):
                 x = share // 4
                 dst = t[:].rearrange("p (w j) -> p w j", j=4)
                 src = raw[k][:].rearrange("p (j w) -> p w j", j=4)
-                copy_on("V", dst[:, 0:x, :], src[:, 0:x, :])
+                copy_on(
+                    "V",
+                    t[:, 0 : 4 * x].rearrange("p (c i j) -> p c j i", i=4, j=4),
+                    raw[k][:].rearrange("p (j c i) -> p c j i", j=4, i=4)[:, 0 : x // 4],
+                )
                 copy_on("S", dst[:, x:1024, :], src[:, x:1024, :])
                 load()
             else:
                 x = share // 8
                 dst = t[:].rearrange("p (c h j) -> p c h j", c=2, j=4)
                 src = raw[k][:].rearrange("p (c j h) -> p c h j", c=2, j=4)
-                copy_on("V", dst[:, :, 0:x, :], src[:, :, 0:x, :])
+                copy_on(
+                    "V",
+                    t[:].rearrange("p (c b i j) -> p c b j i", c=2, i=4, j=4)[:, :, 0 : x // 4],
+                    raw[k][:].rearrange("p (c j b i) -> p c b j i", c=2, j=4, i=4)[:, :, 0 : x // 4],
+                )
                 copy_on("S", dst[:, :, x:512, :], src[:, :, x:512, :])
                 load()
 
@@ -141,7 +149,8 @@ def tile_bertmoeexpertpool_kernel(tc, hidden_states, Wi, bi, Wo, bo, out):
                 return
             t = act.tile([P, 2048], BF16, name="grp_a", tag="grp_a", align_bytes=64)
             nc.vector.tensor_copy(
-                out=t[:].rearrange("p (c n j) -> p c n j", c=2, j=4), in_=gelu_out[k][:].rearrange("p c j n -> p c n j")
+                out=t[:].rearrange("p (c b i j) -> p c b j i", c=2, i=4, j=4),
+                in_=gelu_out[k][:].rearrange("p c j (b i) -> p c b j i", i=4),
             )
             grouped[("a", k)] = t
 

@@ -17,8 +17,8 @@ FLOPS = 2 * E * N * H * F * 2
 
 K_UNITS = 24
 RAW_BUFS = 10
-SPLIT = [1920,2560,3136,2880,1024,2048]
-SPLIT_AT = {1: 3200, 2: 3200, 20: 3136, 21: 2944, 23: 1920}
+SPLIT = [1792,2432,3008,2752,896,1920]
+SPLIT_AT = {1: 3072, 2: 3072, 20: 3008, 21: 2816, 23: 1792}
 HEAD = ["V","S","V","V"]
 
 
@@ -97,7 +97,11 @@ def tile_bertmoeexpertpool_kernel(tc, hidden_states, Wi, bi, Wo, bo, out):
                     t[:, 0 : 4 * x].rearrange("p (c i j) -> p c j i", i=4, j=4),
                     raw[k][:].rearrange("p (j c i) -> p c j i", j=4, i=4)[:, 0 : x // 4],
                 )
-                copy_on("S", dst[:, x:1024, :], src[:, x:1024, :])
+                copy_on(
+                    "S",
+                    t[:, 4 * x : 4096].rearrange("p (c i j) -> p c j i", i=4, j=4),
+                    raw[k][:].rearrange("p (j c i) -> p c j i", j=4, i=4)[:, x // 4 : 256],
+                )
                 load()
             else:
                 x = share // 8
@@ -108,7 +112,12 @@ def tile_bertmoeexpertpool_kernel(tc, hidden_states, Wi, bi, Wo, bo, out):
                     t[:].rearrange("p (c b i j) -> p c b j i", c=2, i=4, j=4)[:, :, 0 : x // 4],
                     raw[k][:].rearrange("p (c j b i) -> p c b j i", c=2, j=4, i=4)[:, :, 0 : x // 4],
                 )
-                copy_on("S", dst[:, :, x:512, :], src[:, :, x:512, :])
+                for c in range(2):
+                    copy_on(
+                        "S",
+                        t[:].rearrange("p (c b i j) -> p c b j i", c=2, i=4, j=4)[:, c, x // 4 : 128],
+                        raw[k][:].rearrange("p (c j b i) -> p c b j i", c=2, j=4, i=4)[:, c, x // 4 : 128],
+                    )
                 load()
 
         def quantise(pool, key, width, tag):

@@ -35,7 +35,6 @@ def tile_bertmoeexpertpool_kernel(tc, hidden_states, Wi, bi, Wo, bo, out):
         res = ctx.enter_context(tc.tile_pool(name="res", bufs=4))
         ps_h = ctx.enter_context(tc.psum_pool(name="ps_h", bufs=6))
         ps_o = ctx.enter_context(tc.psum_pool(name="ps_o", bufs=2))
-        ctx.enter_context(tc.manual_schedule())
 
         raw = {}
         grouped = {}

@@ -17,8 +17,8 @@ FLOPS = 2 * E * N * H * F * 2
 
 K_UNITS = 24
 RAW_BUFS = 10
-SPLIT = [1792,2432,3008,2752,896,1920]
-SPLIT_AT = {1: 3072, 2: 3072, 20: 3008, 21: 2816, 23: 1792}
+SPLIT = [1984,1984,1984,1984,1984,1984]
+SPLIT_AT = {}
 HEAD = ["V","S","V","V"]
 
 
@@ -30,6 +30,7 @@ def tile_bertmoeexpertpool_kernel(tc, hidden_states, Wi, bi, Wo, bo, out):
         headp = ctx.enter_context(tc.tile_pool(name="head", bufs=4))
         grp = ctx.enter_context(tc.tile_pool(name="grp", bufs=3))
         cod = ctx.enter_context(tc.tile_pool(name="cod", bufs=4))
+        cod_o = ctx.enter_context(tc.tile_pool(name="cod_o", bufs=8))
         cod_a = ctx.enter_context(tc.tile_pool(name="cod_a", bufs=6))
         act = ctx.enter_context(tc.tile_pool(name="act", bufs=3))
         res = ctx.enter_context(tc.tile_pool(name="res", bufs=4))
@@ -119,16 +120,20 @@ def tile_bertmoeexpertpool_kernel(tc, hidden_states, Wi, bi, Wo, bo, out):
                     )
                 load()
 
-        def quantise(pool, key, width, tag):
+        def quantise(pool, key, values, tag):
+            width = values.shape[1] // 4
             words = pool.tile([P, width], U32, name="w_" + tag, tag="w_" + tag, align_bytes=64)
             plane = pool.tile([P, width], U8, name="s_" + tag, tag="s_" + tag, align_bytes=64)
-            nc.vector.quantize_mx(out=words[:].bitcast(FP8X4), scales=plane[:], in_=grouped[key][:])
+            nc.vector.quantize_mx(out=words[:].bitcast(FP8X4), scales=plane[:], in_=values)
             codes[key] = words
             planes[key] = plane
 
         def quant_weights(k):
-            if 0 <= k < K_UNITS:
-                quantise(cod, k, 1024, "w")
+            if is_wi(k):
+                quantise(cod, k, grouped[k][:], "w")
+            elif is_wo(k):
+                for c in range(2):
+                    quantise(cod_o, (k, c), grouped[k][:, c * 2048 : (c + 1) * 2048], "o")
 
         def first_matmul_and_gelu(k):
             if not is_wi(k):
@@ -164,7 +169,7 @@ def tile_bertmoeexpertpool_kernel(tc, hidden_states, Wi, bi, Wo, bo, out):
 
         def quant_inter(k):
             if is_wi(k):
-                quantise(cod_a, ("a", k), 2 * N, "a")
+                quantise(cod_a, ("a", k), grouped[("a", k)][:], "a")
 
         def second_matmul(k):
             if not is_wo(k):
@@ -173,15 +178,15 @@ def tile_bertmoeexpertpool_kernel(tc, hidden_states, Wi, bi, Wo, bo, out):
             if u == 0:
                 for a in range(2):
                     acc[(e, a)] = ps_o.tile([P, H], F32, name="o_ps", tag="o_ps")
-            for a in range(2):
-                for c in range(2):
+            for c in range(2):
+                for a in range(2):
                     toks = slice(c * N + a * P, c * N + (a + 1) * P)
                     nc.tensor.matmul_mx(
                         out=acc[(e, a)][:],
                         lhsT=codes[("a", k - 3)][:, toks].bitcast(FP8X4),
                         lhsT_scale=planes[("a", k - 3)][:, toks],
-                        rhs=codes[k][:, c * H : (c + 1) * H].bitcast(FP8X4),
-                        rhs_scale=planes[k][:, c * H : (c + 1) * H],
+                        rhs=codes[(k, c)][:].bitcast(FP8X4),
+                        rhs_scale=planes[(k, c)][:],
                         start=(u == 0 and c == 0),
                         stop=(u == 2 and c == 1),
                     )
@@ -193,8 +198,7 @@ def tile_bertmoeexpertpool_kernel(tc, hidden_states, Wi, bi, Wo, bo, out):
             for a in range(2):
                 o_sb = res.tile([P, H], F32, name="o_sb", tag="o_sb")
                 nc.vector.tensor_tensor(out=o_sb[:], in0=acc[(e, a)][:], in1=bo_bc[:, e * H : (e + 1) * H], op=ALU.add)
-                queue = nc.sync if e == E - 1 else nc.gpsimd
-                queue.dma_start(out=out[e, a * P : (a + 1) * P, :], in_=o_sb[:])
+                nc.sync.dma_start(out=out[e, a * P : (a + 1) * P, :], in_=o_sb[:])
 
         for q in range(4):
             piece = headp.tile([P, 4, 256], BF16, name="piece", tag="piece")

@@ -17,7 +17,7 @@ FLOPS = 2 * E * N * H * F * 2
 
 K_UNITS = 24
 RAW_BUFS = 10
-SPLIT = [1984,1984,1984,1984,1984,1984]
+SPLIT = [2112,2112,2112,2112,2112,2112]
 SPLIT_AT = {}
 HEAD = ["V","S","V","V"]
 
@@ -210,11 +210,11 @@ def tile_bertmoeexpertpool_kernel(tc, hidden_states, Wi, bi, Wo, bo, out):
         bi_rows = const.tile([P, P], BF16, name="bi_rows")
         nc.vector.memset(bi_rows[:], 0.0)
         nc.sync.dma_start(out=bi_rows[0:96, :], in_=bi.rearrange("e (t p) -> (e t) p", p=P))
-        load()
-        load()
+        for s in range(6):
+            load()
         bo_bc = const.tile([P, E * H], BF16, name="bo_bc")
         nc.sync.dma_start(out=bo_bc[:], in_=bo.rearrange("e h -> (e h)").partition_broadcast(P))
-        for s in range(RAW_BUFS - 2):
+        for s in range(RAW_BUFS - 6):
             load()
 
         ident = const.tile([P, P], F32, name="ident")

from contextlib import ExitStack

import concourse.mybir as mybir
from concourse.masks import make_identity

F32 = mybir.dt.float32
BF16 = mybir.dt.bfloat16
U32 = mybir.dt.uint32
U8 = mybir.dt.uint8
FP8X4 = mybir.dt.float8_e4m3fn_x4
ACT = mybir.ActivationFunctionType
ALU = mybir.AluOpType

E, H, F, N = 4, 512, 3072, 256
P = 128
FLOPS = 2 * E * N * H * F * 2

K_UNITS = 24
RAW_BUFS = 10
SPLIT = [2112,2112,2112,2112,2112,2112]
SPLIT_AT = {}
HEAD = ["V","S","V","V"]


def tile_bertmoeexpertpool_kernel(tc, hidden_states, Wi, bi, Wo, bo, out):
    nc = tc.nc
    with ExitStack() as ctx:
        const = ctx.enter_context(tc.tile_pool(name="const", bufs=1))
        rawp = ctx.enter_context(tc.tile_pool(name="raw", bufs=RAW_BUFS))
        headp = ctx.enter_context(tc.tile_pool(name="head", bufs=4))
        grp = ctx.enter_context(tc.tile_pool(name="grp", bufs=3))
        cod = ctx.enter_context(tc.tile_pool(name="cod", bufs=4))
        cod_o = ctx.enter_context(tc.tile_pool(name="cod_o", bufs=8))
        cod_a = ctx.enter_context(tc.tile_pool(name="cod_a", bufs=6))
        act = ctx.enter_context(tc.tile_pool(name="act", bufs=3))
        res = ctx.enter_context(tc.tile_pool(name="res", bufs=4))
        ps_h = ctx.enter_context(tc.psum_pool(name="ps_h", bufs=6))
        ps_o = ctx.enter_context(tc.psum_pool(name="ps_o", bufs=2))

        raw = {}
        grouped = {}
        codes = {}
        planes = {}
        gelu_out = {}
        acc = {}
        next_load = [0]

        def is_wi(k):
            return 0 <= k < K_UNITS and k % 6 < 3

        def is_wo(k):
            return 0 <= k < K_UNITS and k % 6 >= 3

        def wi_rows(k):
            return Wi[k // 6].rearrange("(p j) f -> p j f", j=4)

        def load():
            k = next_load[0]
            next_load[0] += 1
            if k >= K_UNITS:
                return
            e, u = k // 6, k % 3
            t = rawp.tile([P, 4096], BF16, name="raw_t", tag="raw")
            if is_wi(k):
                nc.sync.dma_start(
                    out=t[:].rearrange("p (j w) -> p j w", j=4), in_=wi_rows(k)[:, :, u * 1024 : (u + 1) * 1024]
                )
            else:
                nc.sync.dma_start(
                    out=t[:].rearrange("p (r h) -> p r h", r=8),
                    in_=Wo[e, u * 1024 : (u + 1) * 1024, :].rearrange("(r p) h -> p r h", p=P),
                )
            raw[k] = t

        def copy_on(engine, dst, src):
            if engine == "V":
                nc.vector.tensor_copy(out=dst, in_=src)
            else:
                nc.scalar.copy(out=dst, in_=src)

        def regroup(k):
            if k < 0 or k >= K_UNITS:
                return
            t = grp.tile([P, 4096], BF16, name="grp_t", tag="grp_t", align_bytes=64)
            grouped[k] = t
            share = SPLIT_AT.get(k, SPLIT[k % 6])
            if k == 0:
                dst = t[:].rearrange("p (w j) -> p w j", j=4)
                for q in range(4):
                    copy_on(HEAD[q], dst[:, q * 256 : (q + 1) * 256, :], raw[(0, q)][:].rearrange("p j w -> p w j"))
            elif is_wi(k):
                x = share // 4
                dst = t[:].rearrange("p (w j) -> p w j", j=4)
                src = raw[k][:].rearrange("p (j w) -> p w j", j=4)
                copy_on(
                    "V",
                    t[:, 0 : 4 * x].rearrange("p (c i j) -> p c j i", i=4, j=4),
                    raw[k][:].rearrange("p (j c i) -> p c j i", j=4, i=4)[:, 0 : x // 4],
                )
                copy_on(
                    "S",
                    t[:, 4 * x : 4096].rearrange("p (c i j) -> p c j i", i=4, j=4),
                    raw[k][:].rearrange("p (j c i) -> p c j i", j=4, i=4)[:, x // 4 : 256],
                )
                load()
            else:
                x = share // 8
                dst = t[:].rearrange("p (c h j) -> p c h j", c=2, j=4)
                src = raw[k][:].rearrange("p (c j h) -> p c h j", c=2, j=4)
                copy_on(
                    "V",
                    t[:].rearrange("p (c b i j) -> p c b j i", c=2, i=4, j=4)[:, :, 0 : x // 4],
                    raw[k][:].rearrange("p (c j b i) -> p c b j i", c=2, j=4, i=4)[:, :, 0 : x // 4],
                )
                for c in range(2):
                    copy_on(
                        "S",
                        t[:].rearrange("p (c b i j) -> p c b j i", c=2, i=4, j=4)[:, c, x // 4 : 128],
                        raw[k][:].rearrange("p (c j b i) -> p c b j i", c=2, j=4, i=4)[:, c, x // 4 : 128],
                    )
                load()

        def quantise(pool, key, values, tag):
            width = values.shape[1] // 4
            words = pool.tile([P, width], U32, name="w_" + tag, tag="w_" + tag, align_bytes=64)
            plane = pool.tile([P, width], U8, name="s_" + tag, tag="s_" + tag, align_bytes=64)
            nc.vector.quantize_mx(out=words[:].bitcast(FP8X4), scales=plane[:], in_=values)
            codes[key] = words
            planes[key] = plane

        def quant_weights(k):
            if is_wi(k):
                quantise(cod, k, grouped[k][:], "w")
            elif is_wo(k):
                for c in range(2):
                    quantise(cod_o, (k, c), grouped[k][:, c * 2048 : (c + 1) * 2048], "o")

        def first_matmul_and_gelu(k):
            if not is_wi(k):
                return
            t = act.tile([P, 2, 4, N], BF16, name="gelu_t", tag="gelu_t")
            for i in range(8):
                cols = slice(i * P, (i + 1) * P)
                h_ps = ps_h.tile([P, N], F32, name="h_ps", tag="h_ps")
                nc.tensor.matmul_mx(
                    out=h_ps[:],
                    lhsT=codes[k][:, cols].bitcast(FP8X4),
                    lhsT_scale=planes[k][:, cols],
                    rhs=x_words[:].bitcast(FP8X4),
                    rhs_scale=x_plane[:],
                    start=True,
                    stop=True,
                )
                col = (k // 6) * 24 + (k % 3) * 8 + i
                nc.scalar.activation(
                    out=t[:, i // 4, i % 4, :], in_=h_ps[:], func=ACT.Gelu, bias=bi_t[:, col : col + 1], scale=1.0
                )
            gelu_out[k] = t

        def regroup_inter(k):
            if not is_wi(k):
                return
            t = act.tile([P, 2048], BF16, name="grp_a", tag="grp_a", align_bytes=64)
            nc.vector.tensor_copy(
                out=t[:].rearrange("p (c b i j) -> p c b j i", c=2, i=4, j=4),
                in_=gelu_out[k][:].rearrange("p c j (b i) -> p c b j i", i=4),
            )
            grouped[("a", k)] = t

        def quant_inter(k):
            if is_wi(k):
                quantise(cod_a, ("a", k), grouped[("a", k)][:], "a")

        def second_matmul(k):
            if not is_wo(k):
                return
            e, u = k // 6, k % 3
            if u == 0:
                for a in range(2):
                    acc[(e, a)] = ps_o.tile([P, H], F32, name="o_ps", tag="o_ps")
            for c in range(2):
                for a in range(2):
                    toks = slice(c * N + a * P, c * N + (a + 1) * P)
                    nc.tensor.matmul_mx(
                        out=acc[(e, a)][:],
                        lhsT=codes[("a", k - 3)][:, toks].bitcast(FP8X4),
                        lhsT_scale=planes[("a", k - 3)][:, toks],
                        rhs=codes[(k, c)][:].bitcast(FP8X4),
                        rhs_scale=planes[(k, c)][:],
                        start=(u == 0 and c == 0),
                        stop=(u == 2 and c == 1),
                    )

        def add_bo_and_store(k):
            if not (is_wo(k) and k % 6 == 5):
                return
            e = k // 6
            for a in range(2):
                o_sb = res.tile([P, H], F32, name="o_sb", tag="o_sb")
                nc.vector.tensor_tensor(out=o_sb[:], in0=acc[(e, a)][:], in1=bo_bc[:, e * H : (e + 1) * H], op=ALU.add)
                nc.sync.dma_start(out=out[e, a * P : (a + 1) * P, :], in_=o_sb[:])

        for q in range(4):
            piece = headp.tile([P, 4, 256], BF16, name="piece", tag="piece")
            nc.sync.dma_start(out=piece[:], in_=wi_rows(0)[:, :, q * 256 : (q + 1) * 256])
            raw[(0, q)] = piece
        next_load[0] = 1
        x_sb = const.tile([P, 2, H], BF16, name="x_sb")
        nc.sync.dma_start(out=x_sb[:], in_=hidden_states.rearrange("(a p) k -> p a k", p=P))
        bi_rows = const.tile([P, P], BF16, name="bi_rows")
        nc.vector.memset(bi_rows[:], 0.0)
        nc.sync.dma_start(out=bi_rows[0:96, :], in_=bi.rearrange("e (t p) -> (e t) p", p=P))
        for s in range(6):
            load()
        bo_bc = const.tile([P, E * H], BF16, name="bo_bc")
        nc.sync.dma_start(out=bo_bc[:], in_=bo.rearrange("e h -> (e h)").partition_broadcast(P))
        for s in range(RAW_BUFS - 6):
            load()

        ident = const.tile([P, P], F32, name="ident")
        make_identity(nc, ident[:])
        warm = const.tile([P, 1], F32, name="warm")
        nc.vector.memset(warm[:], 0.0)
        nc.scalar.activation(out=warm[:], in_=warm[:], func=ACT.Gelu)

        x_grp = const.tile([P, 4 * N], BF16, name="x_grp", align_bytes=64)
        x_words = const.tile([P, N], U32, name="x_words", align_bytes=64)
        x_plane = const.tile([P, N], U8, name="x_plane", align_bytes=64)
        bi_f = const.tile([P, P], F32, name="bi_f")
        bi_t = const.tile([P, P], F32, name="bi_t")

        def small_operands():
            x_ps = ps_o.tile([P, 2, N], F32, name="x_ps", tag="o_ps")
            for a in range(2):
                pairs = x_sb[:, a, :].bitcast(F32).rearrange("p (q u) -> p u q", u=2)
                for u in range(2):
                    nc.tensor.transpose(x_ps[:, u, a * P : (a + 1) * P], pairs[:, u, :], ident[:])
            nc.vector.tensor_copy(
                out=x_grp[:].bitcast(F32).rearrange("p (n u) -> p n u", u=2), in_=x_ps[:].rearrange("p u n -> p n u")
            )
            nc.vector.tensor_copy(out=bi_f[:], in_=bi_rows[:])
            nc.vector.quantize_mx(out=x_words[:].bitcast(FP8X4), scales=x_plane[:], in_=x_grp[:])
            bi_ps = ps_h.tile([P, P], F32, name="bi_ps", tag="h_ps")
            nc.tensor.transpose(bi_ps[:], bi_f[:], ident[:])
            nc.vector.tensor_copy(out=bi_t[:], in_=bi_ps[:])

        for k in range(K_UNITS + 3):
            if k == 1:
                small_operands()
            quant_weights(k - 1)
            regroup_inter(k - 2)
            regroup(k)
            first_matmul_and_gelu(k - 1)
            second_matmul(k - 1)
            quant_inter(k - 2)
            add_bo_and_store(k - 2)
